import numpy as np
import ml_dtypes


def mxq(x, axis, fmt="e4m3"):
    dtype, down = {"e4m3": (ml_dtypes.float8_e4m3fn, 7), "e5m2": (ml_dtypes.float8_e5m2, 14)}[fmt]
    v = np.moveaxis(np.asarray(x, np.float32).astype(ml_dtypes.bfloat16).astype(np.float64), axis, -1)
    blocks = v.reshape(v.shape[:-1] + (-1, 32))
    amax = np.abs(blocks).max(-1, keepdims=True)
    byte = np.maximum(np.where(amax > 0, np.frexp(amax)[1] - 1 + 127, 0) - down, 1)
    scale = np.exp2(byte - 127.0)
    codes = (blocks / scale).astype(np.float32).astype(dtype).astype(np.float64)
    return np.moveaxis((codes * scale).reshape(v.shape), -1, axis)


WIDE = False


def mx_kscale(k):
    if not WIDE:
        return np.ones(k)
    levels = np.array([10, -10, 5, -5, 0])
    if k % 512:
        return np.exp2(np.random.permutation(np.resize(levels, k // 32))).repeat(32)
    a = np.empty((k // 512, 16))
    for p in range(k // 512):
        a[p, :8] = np.random.permutation(np.resize(levels, 8))
        for g in range(8):
            far = levels[np.abs(levels - a[p, g]) >= 10]
            a[p, g + 8] = far[np.random.randint(len(far))]
    return np.exp2(a.ravel()).repeat(32)


BF16 = ml_dtypes.bfloat16


def bf(x):
    return np.asarray(x, np.float32).astype(BF16)


def f64(x):
    return np.asarray(x).astype(np.float64)


B, N, E, H, G, D, WIN = 1, 1024, 1024, 8, 4, 128, 512
HK = H // G
HALF = D // 2


def apply_rope(y, cos, sin):
    By, Ny, Hy, Dy = y.shape
    yp = y.reshape(By, Ny, Hy, Dy // 2, 2)
    y0, y1 = yp[..., 0], yp[..., 1]
    c = cos[:, :, None, :]
    s = sin[:, :, None, :]
    r0 = y0 * c - y1 * s
    r1 = y0 * s + y1 * c
    return np.stack([r0, r1], axis=-1).reshape(By, Ny, Hy, Dy)


def draw0():
    s = mx_kscale(E)
    inv_freq = 1.0 / 10000.0 ** (np.arange(HALF) / HALF)
    ang = np.arange(N)[:, None] * inv_freq[None, :]
    return {"x": bf(np.random.standard_normal((B, N, E)) * s),
            "rope_cos": bf(np.broadcast_to(np.cos(ang)[None], (B, N, HALF))),
            "rope_sin": bf(np.broadcast_to(np.sin(ang)[None], (B, N, HALF))),
            "Wq": bf(np.random.standard_normal((E, H * D)) * 1.5 / np.sqrt(E) / s[:, None]),
            "Wk": bf(np.random.standard_normal((E, HK * D)) * 1.5 / np.sqrt(E) / s[:, None]),
            "Wv": bf(np.random.standard_normal((E, HK * D)) / np.sqrt(E) / s[:, None])}


def core(x, rope_cos, rope_sin, Wq, Wk, Wv):
    xq = mxq(f64(x), 2, "e4m3")
    q = (xq @ mxq(f64(Wq), 0, "e4m3")).reshape(B, N, H, D)
    k = (xq @ mxq(f64(Wk), 0, "e4m3")).reshape(B, N, HK, D)
    v = (xq @ mxq(f64(Wv), 0, "e4m3")).reshape(B, N, HK, D)
    q = apply_rope(q, f64(rope_cos), f64(rope_sin))
    k = apply_rope(k, f64(rope_cos), f64(rope_sin))
    return q.transpose(0, 2, 1, 3), k.transpose(0, 2, 1, 3), v.transpose(0, 2, 1, 3)


def e4m3fn_bytes(y):
    return np.clip(np.asarray(y, np.float64), -448.0, 448.0).astype(np.float32).astype(ml_dtypes.float8_e4m3fn).view(np.uint8)


def e4m3fn_values(b):
    return np.asarray(b, np.uint8).view(ml_dtypes.float8_e4m3fn).astype(np.float64)


def setup_inputs():
    d = draw0()
    x0 = np.asarray(d['x']).astype(np.float64)
    s = (np.max(np.abs(x0), axis=(0, 1), keepdims=True) / 448.0).astype(np.float32)
    out = {}
    for k, v in d.items():
        if k == 'x':
            out['x_bytes'] = e4m3fn_bytes(x0 / s.astype(np.float64))
            out['x_scale'] = s
        else:
            out[k] = v
    return out


def reference(x_bytes, x_scale, rope_cos, rope_sin, Wq, Wk, Wv):
    return core(e4m3fn_values(x_bytes) * x_scale.astype(np.float64), rope_cos, rope_sin, Wq, Wk, Wv)

@@ -1,0 +1,252 @@
+from contextlib import ExitStack
+
+import concourse.mybir as mybir
+from concourse.masks import make_identity
+
+FLOPS = 2 * 1024 * 1024 * 1536
+
+F32 = mybir.dt.float32
+BF16 = mybir.dt.bfloat16
+U32 = mybir.dt.uint32
+U8 = mybir.dt.uint8
+FP8 = mybir.dt.float8_e4m3fn
+FP8X4 = mybir.dt.float8_e4m3fn_x4
+MULT = mybir.AluOpType.mult
+ADD = mybir.AluOpType.add
+
+P = 128
+E = 1024
+NT = 8
+HALF = 64
+GPSIMD_INTERLEAVES = ((0, 0), (0, 1), (1, 0))
+VECTOR_ADDS = ((2, 0), (2, 1), (2, 2), (2, 3))
+
+
+def tile_groupedqueryattention_pa_kernel(
+    tc, x_bytes, x_scale, rope_cos, rope_sin, Wq, Wk, Wv, out_0, out_1, out_2
+):
+    nc = tc.nc
+    with ExitStack() as ctx:
+        const = ctx.enter_context(tc.tile_pool(name="const", bufs=1))
+        xc_pool = ctx.enter_context(tc.tile_pool(name="xc_pool", bufs=6))
+        wg_pool = ctx.enter_context(tc.tile_pool(name="wg_pool", bufs=3))
+        u_pool = ctx.enter_context(tc.tile_pool(name="u_pool", bufs=5))
+        uk_pool = ctx.enter_context(tc.tile_pool(name="uk_pool", bufs=4))
+        psum_t = ctx.enter_context(tc.psum_pool(name="psum_t", bufs=3))
+        psum_a = ctx.enter_context(tc.psum_pool(name="psum_a", bufs=5))
+
+        xv = x_bytes.rearrange("o (p i) k -> p (o i) k", i=NT)
+        xb = []
+        for j in range(NT // 2):
+            xb.append(const.tile([P, 2, E], U8, name="xbytes%d" % j))
+
+        def load_x(j):
+            nc.sync.dma_start(out=xb[j][:], in_=xv[:, 2 * j : 2 * j + 2, :])
+
+        def load_x_tile(i):
+            nc.sync.dma_start(out=xb[i // 2][:, i % 2, :], in_=xv[:, i, :])
+
+        w_views = []
+        for w in (Wq, Wk, Wv):
+            w_views.append(w.rearrange("(g p j) w -> g p j w", p=P, j=4))
+        wraw = {}
+        for c in range(3):
+            for g in range(2):
+                wraw[(c, g)] = const.tile([P, 4, 512], BF16, name="wraw%d%d" % (c, g))
+
+        def load_w(c, g):
+            if c < 2:
+                nc.sync.dma_start(out=wraw[(c, g)][:], in_=w_views[0][g][:, :, 512 * c : 512 * (c + 1)])
+            else:
+                nc.sync.dma_start(out=wraw[(c, g)][:, :, 0:256], in_=w_views[1][g])
+                nc.sync.dma_start(out=wraw[(c, g)][:, :, 256:512], in_=w_views[2][g])
+
+        load_x_tile(0)
+        sc4 = const.tile([P, 2, 4], F32, name="sc4")
+        nc.sync.dma_start(out=sc4[:], in_=x_scale.rearrange("o q (g p t) -> p (o q g) t", p=P, t=4))
+        load_x_tile(1)
+        load_x(1)
+        load_w(0, 0)
+        load_w(0, 1)
+        load_x(2)
+        load_x(3)
+        load_w(1, 0)
+        tab = const.tile([P, NT, 4, HALF], BF16, name="tab")
+        cos_v = rope_cos.rearrange("o (p i) f -> p (o i) f", i=NT)
+        sin_v = rope_sin.rearrange("o (p i) f -> p (o i) f", i=NT)
+        nc.sync.dma_start(out=tab[:, :, 1, :], in_=sin_v)
+        nc.sync.dma_start(out=tab[:, :, 0, :], in_=cos_v)
+        nc.sync.dma_start(out=tab[:, :, 3, :], in_=cos_v)
+        load_w(1, 1)
+        load_w(2, 0)
+        load_w(2, 1)
+
+        warm_in = const.tile([P, 1], F32, name="warm_in")
+        warm_out = const.tile([P, 1], F32, name="warm_out")
+        nc.gpsimd.memset(warm_in[:], 0.0)
+        nc.scalar.copy(out=warm_out[:], in_=warm_in[:])
+        ident = const.tile([P, P], F32, name="ident")
+        make_identity(nc, ident[:])
+
+        grouped = []
+        xcodes = []
+        xscl = []
+        for j in range(NT // 2):
+            grouped.append(const.tile([P, 2, E], BF16, name="grouped%d" % j, align_bytes=64))
+            xcodes.append(const.tile([P, 512], U32, name="xcodes%d" % j, align_bytes=64))
+            xscl.append(const.tile([P, 512], U8, name="xscl%d" % j, align_bytes=64))
+        wcodes = []
+        wscl = []
+        for c in range(3):
+            wcodes.append(const.tile([P, 1024], U32, name="wcodes%d" % c, align_bytes=64))
+            wscl.append(const.tile([P, 1024], U8, name="wscl%d" % c, align_bytes=64))
+
+        def interleave_w(c):
+            wg = wg_pool.tile([P, 2, 2048], BF16, name="wg", align_bytes=64)
+            for g in range(2):
+                dst = wg[:, g, :].rearrange("p (x j) -> p x j", j=4)
+                src = wraw[(c, g)][:].rearrange("p j x -> p x j")
+                if (c, g) in GPSIMD_INTERLEAVES:
+                    nc.gpsimd.tensor_scalar(out=dst, in0=src, scalar1=1.0, scalar2=0.0, op0=MULT, op1=ADD)
+                else:
+                    nc.scalar.copy(out=dst, in_=src)
+            return wg
+
+        def quant_w(c, wg):
+            nc.vector.quantize_mx(
+                out=wcodes[c][:].bitcast(FP8X4),
+                scales=wscl[c][:],
+                in_=wg[:].rearrange("p g n -> p (g n)"),
+            )
+
+        def prep_x(i):
+            for g in range(2):
+                xc = xc_pool.tile([P, 512], BF16, name="xc")
+                nc.scalar.copy(out=xc[:], in_=xb[i // 2][:, i % 2, 512 * g : 512 * (g + 1)].bitcast(FP8))
+                words = xc[:].bitcast(F32)
+                xt = psum_t.tile([P, 2, P], F32, name="xt")
+                for u in range(2):
+                    nc.tensor.transpose(xt[:, u, :], words[:, u:256:2], ident[:])
+                nc.vector.tensor_tensor(
+                    out=grouped[i // 2][:, i % 2, 512 * g : 512 * (g + 1)].rearrange(
+                        "p (r u e) -> p r u e", u=2, e=2
+                    ),
+                    in0=xt[:]
+                    .rearrange("p u r -> p (u r)")
+                    .bitcast(BF16)
+                    .rearrange("p (u r e) -> p r u e", u=2, e=2),
+                    in1=sc4[:, g, :]
+                    .rearrange("p (u e) -> p u e", e=2)
+                    .unsqueeze(1)
+                    .to_broadcast([P, P, 2, 2]),
+                    op=MULT,
+                )
+
+        def quant_x(j):
+            nc.vector.quantize_mx(
+                out=xcodes[j][:].bitcast(FP8X4),
+                scales=xscl[j][:],
+                in_=grouped[j][:].rearrange("p a n -> p (a n)"),
+            )
+
+        q_res = []
+        for c in range(2):
+            q_res.append(const.tile([P, 4, NT, P], F32, name="q_res%d" % c))
+        k_res = const.tile([P, 2, NT, P], F32, name="k_res")
+        v_res = const.tile([P, 2, NT, P], F32, name="v_res")
+        q_out = out_0.rearrange("o h (p i) d -> p (o h) i d", i=NT)
+        k_out = out_1.rearrange("o h (p i) d -> p (o h) i d", i=NT)
+        v_out = out_2.rearrange("o h (p i) d -> p (o h) i d", i=NT)
+
+        def products(c, j):
+            heads = 4 if c < 2 else 2
+            width = heads * P
+            if c < 2:
+                u = u_pool.tile([P, 2, 2, 512], F32, name="u")
+            else:
+                u = uk_pool.tile([P, 2, 2, 256], F32, name="uk")
+            for a in range(2):
+                i = 2 * j + a
+                acc = psum_a.tile([P, 512], F32, name="acc")
+                for g in range(2):
+                    xo = a * 256 + g * P
+                    nc.tensor.matmul_mx(
+                        out=acc[:],
+                        lhsT=xcodes[j][:, xo : xo + P].bitcast(FP8X4),
+                        lhsT_scale=xscl[j][:, xo : xo + P],
+                        rhs=wcodes[c][:, 512 * g : 512 * (g + 1)].bitcast(FP8X4),
+                        rhs_scale=wscl[c][:, 512 * g : 512 * (g + 1)],
+                        start=(g == 0),
+                        stop=(g == 1),
+                    )
+                y = acc[:, 0:width].rearrange("p (h q e) -> p h q e", h=heads, e=2)
+                for b in range(2):
+                    nc.vector.tensor_tensor(
+                        out=u[:, a, b, 0:width].rearrange("p (h q e) -> p h q e", h=heads, e=2),
+                        in0=y[:, :, :, b : b + 1].to_broadcast([P, heads, HALF, 2]),
+                        in1=tab[:, i, 2 * b : 2 * b + 2, :]
+                        .rearrange("p e q -> p q e")
+                        .unsqueeze(1)
+                        .to_broadcast([P, heads, HALF, 2]),
+                        op=MULT,
+                    )
+                if c == 2:
+                    nc.scalar.copy(
+                        out=v_res[:, :, i, :], in_=acc[:, 256:512].rearrange("p (h d) -> p h d", h=2)
+                    )
+            if c == 2:
+                rows = slice(2 * j, 2 * j + 2)
+                nc.sync.dma_start(out=v_out[:, :, rows, :], in_=v_res[:, :, rows, :])
+            return u
+
+        def add_and_store(c, j, u):
+            heads = 4 if c < 2 else 2
+            width = heads * P
+            res = q_res[c] if c < 2 else k_res
+            dram = q_out[:, 4 * c : 4 * c + 4] if c < 2 else k_out
+            if (c, j) in VECTOR_ADDS:
+                for a in range(2):
+                    i = 2 * j + a
+                    nc.vector.tensor_tensor(
+                        out=res[:, :, i, :],
+                        in0=u[:, a, 0, 0:width].rearrange("p (h d) -> p h d", h=heads),
+                        in1=u[:, a, 1, 0:width].rearrange("p (h d) -> p h d", h=heads),
+                        op=ADD,
+                    )
+                    nc.sync.dma_start(out=dram[:, :, i, :], in_=res[:, :, i, :])
+            else:
+                rows = slice(2 * j, 2 * j + 2)
+                nc.gpsimd.tensor_tensor(
+                    out=res[:, :, rows, :].rearrange("p h i d -> p i h d"),
+                    in0=u[:, :, 0, 0:width].rearrange("p i (h d) -> p i h d", h=heads),
+                    in1=u[:, :, 1, 0:width].rearrange("p i (h d) -> p i h d", h=heads),
+                    op=ADD,
+                )
+                nc.sync.dma_start(out=dram[:, :, rows, :], in_=res[:, :, rows, :])
+
+        with tc.manual_schedule(engines={mybir.EngineType.DVE}):
+            for i in range(NT):
+                prep_x(i)
+            wgs = []
+            for c in range(3):
+                wgs.append(interleave_w(c))
+            for j in range(NT // 2):
+                quant_x(j)
+            nc.vector.tensor_scalar(
+                out=tab[:, :, 2, :], in0=tab[:, :, 1, :], scalar1=-1.0, scalar2=None, op0=MULT
+            )
+            quant_w(0, wgs[0])
+            quant_w(1, wgs[1])
+
+            late = []
+            for c in range(3):
+                for j in range(NT // 2):
+                    u = products(c, j)
+                    if (c, j) == (0, 0):
+                        quant_w(2, wgs[2])
+                    if (c, j) in VECTOR_ADDS:
+                        late.append((c, j, u))
+                    else:
+                        add_and_store(c, j, u)
+            for c, j, u in late:
+                add_and_store(c, j, u)

@@ -19,7 +19,9 @@ E = 1024
 NT = 8
 HALF = 64
 GPSIMD_INTERLEAVES = ((0, 0), (0, 1), (1, 0))
-VECTOR_ADDS = ((2, 0), (2, 1), (2, 2), (2, 3))
+UNITS = ((0, 0), (0, 1), (0, 2), (0, 3), (1, 0), (1, 1), (1, 2), (2, 0), (1, 3), (2, 1), (2, 2), (2, 3))
+VECTOR_ADDS = ((2, 1), (2, 2), (2, 3))
+TENSOR_ADDS = ((2, 0),)
 
 
 def tile_groupedqueryattention_pa_kernel(
@@ -204,7 +206,21 @@ def tile_groupedqueryattention_pa_kernel(
             width = heads * P
             res = q_res[c] if c < 2 else k_res
             dram = q_out[:, 4 * c : 4 * c + 4] if c < 2 else k_out
-            if (c, j) in VECTOR_ADDS:
+            if (c, j) in TENSOR_ADDS:
+                ksum = psum_t.tile([P, 2, 256], F32, name="xt")
+                for a in range(2):
+                    i = 2 * j + a
+                    for b in range(2):
+                        nc.tensor.matmul(
+                            out=ksum[:, a, :],
+                            lhsT=ident[:],
+                            rhs=u[:, a, b, 0:width],
+                            start=(b == 0),
+                            stop=(b == 1),
+                        )
+                    nc.scalar.copy(out=res[:, :, i, :], in_=ksum[:, a, :].rearrange("p (h d) -> p h d", h=heads))
+                    nc.sync.dma_start(out=dram[:, :, i, :], in_=res[:, :, i, :])
+            elif (c, j) in VECTOR_ADDS:
                 for a in range(2):
                     i = 2 * j + a
                     nc.vector.tensor_tensor(
@@ -239,14 +255,18 @@ def tile_groupedqueryattention_pa_kernel(
             quant_w(1, wgs[1])
 
             late = []
-            for c in range(3):
-                for j in range(NT // 2):
+            for c, j in UNITS:
+                if True:
                     u = products(c, j)
                     if (c, j) == (0, 0):
                         quant_w(2, wgs[2])
                     if (c, j) in VECTOR_ADDS:
                         late.append((c, j, u))
+                    elif (c, j) in TENSOR_ADDS:
+                        held = (c, j, u)
                     else:
                         add_and_store(c, j, u)
+                    if (c, j) == (1, 3):
+                        add_and_store(*held)
             for c, j, u in late:
                 add_and_store(c, j, u)

@@ -20,6 +20,7 @@ NT = 8
 HALF = 64
 GPSIMD_INTERLEAVES = ((0, 0), (0, 1), (1, 0))
 UNITS = ((0, 0), (0, 1), (0, 2), (0, 3), (1, 0), (1, 1), (1, 2), (2, 0), (1, 3), (2, 1), (2, 2), (2, 3))
+V_BEHIND = {(0, 1): 0, (0, 2): 1, (0, 3): 2, (1, 0): 3}
 VECTOR_ADDS = ((2, 1), (2, 2), (2, 3))
 TENSOR_ADDS = ((2, 0),)
 
@@ -173,11 +174,11 @@ def tile_groupedqueryattention_pa_kernel(
                 for g in range(2):
                     xo = a * 256 + g * P
                     nc.tensor.matmul_mx(
-                        out=acc[:],
+                        out=acc[:, 0:width],
                         lhsT=xcodes[j][:, xo : xo + P].bitcast(FP8X4),
                         lhsT_scale=xscl[j][:, xo : xo + P],
-                        rhs=wcodes[c][:, 512 * g : 512 * (g + 1)].bitcast(FP8X4),
-                        rhs_scale=wscl[c][:, 512 * g : 512 * (g + 1)],
+                        rhs=wcodes[c][:, 512 * g : 512 * g + width].bitcast(FP8X4),
+                        rhs_scale=wscl[c][:, 512 * g : 512 * g + width],
                         start=(g == 0),
                         stop=(g == 1),
                     )
@@ -192,14 +193,28 @@ def tile_groupedqueryattention_pa_kernel(
                         .to_broadcast([P, heads, HALF, 2]),
                         op=MULT,
                     )
-                if c == 2:
-                    nc.scalar.copy(
-                        out=v_res[:, :, i, :], in_=acc[:, 256:512].rearrange("p (h d) -> p h d", h=2)
-                    )
-            if c == 2:
-                rows = slice(2 * j, 2 * j + 2)
-                nc.sync.dma_start(out=v_out[:, :, rows, :], in_=v_res[:, :, rows, :])
             return u
+
+        def v_unit(j):
+            vacc = psum_a.tile([P, 512], F32, name="acc")
+            for a in range(2):
+                for g in range(2):
+                    xo = a * 256 + g * P
+                    nc.tensor.matmul_mx(
+                        out=vacc[:, 256 * a : 256 * (a + 1)],
+                        lhsT=xcodes[j][:, xo : xo + P].bitcast(FP8X4),
+                        lhsT_scale=xscl[j][:, xo : xo + P],
+                        rhs=wcodes[2][:, 512 * g + 256 : 512 * (g + 1)].bitcast(FP8X4),
+                        rhs_scale=wscl[2][:, 512 * g + 256 : 512 * (g + 1)],
+                        start=(g == 0),
+                        stop=(g == 1),
+                    )
+            rows = slice(2 * j, 2 * j + 2)
+            nc.scalar.copy(
+                out=v_res[:, :, rows, :].rearrange("p h i d -> p i h d"),
+                in_=vacc[:].rearrange("p (i h d) -> p i h d", i=2, h=2),
+            )
+            nc.sync.dma_start(out=v_out[:, :, rows, :], in_=v_res[:, :, rows, :])
 
         def add_and_store(c, j, u):
             heads = 4 if c < 2 else 2
@@ -268,5 +283,7 @@ def tile_groupedqueryattention_pa_kernel(
                         add_and_store(c, j, u)
                     if (c, j) == (1, 3):
                         add_and_store(*held)
+                    if (c, j) in V_BEHIND:
+                        v_unit(V_BEHIND[(c, j)])
             for c, j, u in late:
                 add_and_store(c, j, u)

@@ -18,11 +18,13 @@ P = 128
 E = 1024
 NT = 8
 HALF = 64
-GPSIMD_INTERLEAVES = ((0, 0), (0, 1), (1, 0))
-UNITS = ((0, 0), (0, 1), (0, 2), (0, 3), (1, 0), (1, 1), (1, 2), (2, 0), (1, 3), (2, 1), (2, 2), (2, 3))
-V_BEHIND = {(0, 1): 0, (0, 2): 1, (0, 3): 2, (1, 0): 3}
-VECTOR_ADDS = ((2, 1), (2, 2), (2, 3))
-TENSOR_ADDS = ((2, 0),)
+UNITS = ((0, 0), (0, 1), (0, 2), (1, 0), (1, 1), (1, 2), (2, 0), (0, 3), (1, 3), (2, 1), (2, 2), (2, 3))
+V_BEHIND = {(1, 1): 0, (1, 2): 1, (2, 0): 2, (0, 3): 3}
+VECTOR_ADDS = ((2, 3),)
+TENSOR_ADDS = ((2, 0), (2, 1))
+COVER_TILE = 5
+TENSOR_LAG = 2
+PLANE_PAIR = 3
 
 
 def tile_groupedqueryattention_pa_kernel(
@@ -34,6 +36,7 @@ def tile_groupedqueryattention_pa_kernel(
         xc_pool = ctx.enter_context(tc.tile_pool(name="xc_pool", bufs=6))
         wg_pool = ctx.enter_context(tc.tile_pool(name="wg_pool", bufs=3))
         u_pool = ctx.enter_context(tc.tile_pool(name="u_pool", bufs=5))
+        plane_pool = ctx.enter_context(tc.tile_pool(name="plane_pool", bufs=2))
         uk_pool = ctx.enter_context(tc.tile_pool(name="uk_pool", bufs=4))
         psum_t = ctx.enter_context(tc.psum_pool(name="psum_t", bufs=3))
         psum_a = ctx.enter_context(tc.psum_pool(name="psum_a", bufs=5))
@@ -72,17 +75,17 @@ def tile_groupedqueryattention_pa_kernel(
         load_w(0, 0)
         load_w(0, 1)
         load_x(2)
-        load_x(3)
         load_w(1, 0)
+        load_w(1, 1)
+        load_w(2, 0)
         tab = const.tile([P, NT, 4, HALF], BF16, name="tab")
         cos_v = rope_cos.rearrange("o (p i) f -> p (o i) f", i=NT)
         sin_v = rope_sin.rearrange("o (p i) f -> p (o i) f", i=NT)
         nc.sync.dma_start(out=tab[:, :, 1, :], in_=sin_v)
         nc.sync.dma_start(out=tab[:, :, 0, :], in_=cos_v)
         nc.sync.dma_start(out=tab[:, :, 3, :], in_=cos_v)
-        load_w(1, 1)
-        load_w(2, 0)
         load_w(2, 1)
+        load_x(3)
 
         warm_in = const.tile([P, 1], F32, name="warm_in")
         warm_out = const.tile([P, 1], F32, name="warm_out")
@@ -104,45 +107,75 @@ def tile_groupedqueryattention_pa_kernel(
             wcodes.append(const.tile([P, 1024], U32, name="wcodes%d" % c, align_bytes=64))
             wscl.append(const.tile([P, 1024], U8, name="wscl%d" % c, align_bytes=64))
 
-        def interleave_w(c):
-            wg = wg_pool.tile([P, 2, 2048], BF16, name="wg", align_bytes=64)
-            for g in range(2):
-                dst = wg[:, g, :].rearrange("p (x j) -> p x j", j=4)
-                src = wraw[(c, g)][:].rearrange("p j x -> p x j")
-                if (c, g) in GPSIMD_INTERLEAVES:
-                    nc.gpsimd.tensor_scalar(out=dst, in0=src, scalar1=1.0, scalar2=0.0, op0=MULT, op1=ADD)
-                else:
-                    nc.scalar.copy(out=dst, in_=src)
-            return wg
+        def interleave_w(engine, c, g, dst):
+            out = dst.rearrange("p (x j) -> p x j", j=4)
+            src = wraw[(c, g)][:].rearrange("p j x -> p x j")
+            if engine is nc.gpsimd:
+                nc.gpsimd.tensor_scalar(out=out, in0=src, scalar1=1.0, scalar2=0.0, op0=MULT, op1=ADD)
+            else:
+                nc.scalar.copy(out=out, in_=src)
 
-        def quant_w(c, wg):
-            nc.vector.quantize_mx(
-                out=wcodes[c][:].bitcast(FP8X4),
-                scales=wscl[c][:],
-                in_=wg[:].rearrange("p g n -> p (g n)"),
+        def quant_w(c, g0, passes, src):
+            cols = slice(512 * g0, 512 * (g0 + passes))
+            nc.vector.quantize_mx(out=wcodes[c][:, cols].bitcast(FP8X4), scales=wscl[c][:, cols], in_=src)
+
+        def cast_x(i, g):
+            xc = xc_pool.tile([P, 512], BF16, name="xc")
+            src = xb[i // 2][:, i % 2, 512 * g : 512 * (g + 1)].bitcast(FP8)
+            if (i, g) == (0, 0):
+                nc.vector.tensor_copy(out=xc[:], in_=src)
+            else:
+                nc.scalar.copy(out=xc[:], in_=src)
+            return xc
+
+        def turn_x(i, g):
+            words = cast_x(i, g)[:].bitcast(F32)
+            xt = psum_t.tile([P, 2, P], F32, name="xt")
+            for u in range(2):
+                nc.tensor.transpose(xt[:, u, :], words[:, u:256:2], ident[:])
+            return xt
+
+        def scale_x(i, g, xt):
+            nc.vector.tensor_tensor(
+                out=grouped[i // 2][:, i % 2, 512 * g : 512 * (g + 1)].rearrange("p (r u e) -> p r u e", u=2, e=2),
+                in0=xt[:]
+                .rearrange("p u r -> p (u r)")
+                .bitcast(BF16)
+                .rearrange("p (u r e) -> p r u e", u=2, e=2),
+                in1=sc4[:, g, :]
+                .rearrange("p (u e) -> p u e", e=2)
+                .unsqueeze(1)
+                .to_broadcast([P, P, 2, 2]),
+                op=MULT,
             )
 
-        def prep_x(i):
+        def prep_x_planes(j):
+            planes = []
+            xts = []
             for g in range(2):
-                xc = xc_pool.tile([P, 512], BF16, name="xc")
-                nc.scalar.copy(out=xc[:], in_=xb[i // 2][:, i % 2, 512 * g : 512 * (g + 1)].bitcast(FP8))
-                words = xc[:].bitcast(F32)
-                xt = psum_t.tile([P, 2, P], F32, name="xt")
-                for u in range(2):
-                    nc.tensor.transpose(xt[:, u, :], words[:, u:256:2], ident[:])
-                nc.vector.tensor_tensor(
-                    out=grouped[i // 2][:, i % 2, 512 * g : 512 * (g + 1)].rearrange(
-                        "p (r u e) -> p r u e", u=2, e=2
-                    ),
-                    in0=xt[:]
-                    .rearrange("p u r -> p (u r)")
-                    .bitcast(BF16)
-                    .rearrange("p (u r e) -> p r u e", u=2, e=2),
-                    in1=sc4[:, g, :]
-                    .rearrange("p (u e) -> p u e", e=2)
-                    .unsqueeze(1)
-                    .to_broadcast([P, P, 2, 2]),
-                    op=MULT,
+                xt = psum_t.tile([P, 2, 2, P], F32, name="xt")
+                for a in range(2):
+                    words = cast_x(2 * j + a, g)[:].bitcast(F32)
+                    for u in range(2):
+                        nc.tensor.transpose(xt[:, u, a, :], words[:, u:256:2], ident[:])
+                xts.append(xt)
+            for g in range(2):
+                plane = plane_pool.tile([P, 4, 2, P], BF16, name="plane")
+                halves = (
+                    xts[g][:].rearrange("p u a r -> p (u a r)").bitcast(BF16).rearrange("p (u s e) -> p u e s", u=2, e=2)
+                )
+                for t in range(4):
+                    nc.scalar.activation(
+                        out=plane[:, t].rearrange("p a r -> p (a r)"),
+                        in_=halves[:, t // 2, t % 2, :],
+                        func=mybir.ActivationFunctionType.Copy,
+                        scale=sc4[:, g, t : t + 1],
+                    )
+                planes.append(plane)
+            for g in range(2):
+                nc.scalar.copy(
+                    out=grouped[j][:, :, 512 * g : 512 * (g + 1)].rearrange("p a (r t) -> p a r t", t=4),
+                    in_=planes[g][:].rearrange("p t a r -> p a r t"),
                 )
 
         def quant_x(j):
@@ -161,15 +194,10 @@ def tile_groupedqueryattention_pa_kernel(
         k_out = out_1.rearrange("o h (p i) d -> p (o h) i d", i=NT)
         v_out = out_2.rearrange("o h (p i) d -> p (o h) i d", i=NT)
 
-        def products(c, j):
-            heads = 4 if c < 2 else 2
-            width = heads * P
-            if c < 2:
-                u = u_pool.tile([P, 2, 2, 512], F32, name="u")
-            else:
-                u = uk_pool.tile([P, 2, 2, 256], F32, name="uk")
+        def passes(c, j):
+            width = 512 if c < 2 else 256
+            accs = []
             for a in range(2):
-                i = 2 * j + a
                 acc = psum_a.tile([P, 512], F32, name="acc")
                 for g in range(2):
                     xo = a * 256 + g * P
@@ -182,7 +210,19 @@ def tile_groupedqueryattention_pa_kernel(
                         start=(g == 0),
                         stop=(g == 1),
                     )
-                y = acc[:, 0:width].rearrange("p (h q e) -> p h q e", h=heads, e=2)
+                accs.append(acc)
+            return accs
+
+        def products(c, j, accs):
+            heads = 4 if c < 2 else 2
+            width = heads * P
+            if c < 2:
+                u = u_pool.tile([P, 2, 2, 512], F32, name="u")
+            else:
+                u = uk_pool.tile([P, 2, 2, 256], F32, name="uk")
+            for a in range(2):
+                i = 2 * j + a
+                y = accs[a][:, 0:width].rearrange("p (h q e) -> p h q e", h=heads, e=2)
                 for b in range(2):
                     nc.vector.tensor_tensor(
                         out=u[:, a, b, 0:width].rearrange("p (h q e) -> p h q e", h=heads, e=2),
@@ -216,26 +256,20 @@ def tile_groupedqueryattention_pa_kernel(
             )
             nc.sync.dma_start(out=v_out[:, :, rows, :], in_=v_res[:, :, rows, :])
 
+        def tensor_add(c, j, u, a):
+            i = 2 * j + a
+            ksum = psum_t.tile([P, 256], F32, name="xt")
+            for b in range(2):
+                nc.tensor.matmul(out=ksum[:], lhsT=ident[:], rhs=u[:, a, b, :], start=(b == 0), stop=(b == 1))
+            nc.scalar.copy(out=k_res[:, :, i, :], in_=ksum[:].rearrange("p (h d) -> p h d", h=2))
+            nc.sync.dma_start(out=k_out[:, :, i, :], in_=k_res[:, :, i, :])
+
         def add_and_store(c, j, u):
             heads = 4 if c < 2 else 2
             width = heads * P
             res = q_res[c] if c < 2 else k_res
             dram = q_out[:, 4 * c : 4 * c + 4] if c < 2 else k_out
-            if (c, j) in TENSOR_ADDS:
-                ksum = psum_t.tile([P, 2, 256], F32, name="xt")
-                for a in range(2):
-                    i = 2 * j + a
-                    for b in range(2):
-                        nc.tensor.matmul(
-                            out=ksum[:, a, :],
-                            lhsT=ident[:],
-                            rhs=u[:, a, b, 0:width],
-                            start=(b == 0),
-                            stop=(b == 1),
-                        )
-                    nc.scalar.copy(out=res[:, :, i, :], in_=ksum[:, a, :].rearrange("p (h d) -> p h d", h=heads))
-                    nc.sync.dma_start(out=dram[:, :, i, :], in_=res[:, :, i, :])
-            elif (c, j) in VECTOR_ADDS:
+            if (c, j) in VECTOR_ADDS:
                 for a in range(2):
                     i = 2 * j + a
                     nc.vector.tensor_tensor(
@@ -255,35 +289,60 @@ def tile_groupedqueryattention_pa_kernel(
                 )
                 nc.sync.dma_start(out=dram[:, :, rows, :], in_=res[:, :, rows, :])
 
-        with tc.manual_schedule(engines={mybir.EngineType.DVE}):
-            for i in range(NT):
-                prep_x(i)
-            wgs = []
-            for c in range(3):
-                wgs.append(interleave_w(c))
-            for j in range(NT // 2):
-                quant_x(j)
+        engines = mybir.EngineType
+        with tc.manual_schedule(engines={engines.DVE, engines.Activation, engines.PE, engines.Pool}):
+            for i in range(COVER_TILE):
+                for g in range(2):
+                    scale_x(i, g, turn_x(i, g))
+            cover = [turn_x(COVER_TILE, g) for g in range(2)]
+            wg0 = wg_pool.tile([P, 4096], BF16, name="wg", align_bytes=64)
+            wg1 = wg_pool.tile([P, 4096], BF16, name="wg", align_bytes=64)
+            wg21 = wg_pool.tile([P, 2048], BF16, name="wg", align_bytes=64)
+            for g in range(2):
+                interleave_w(nc.gpsimd, 0, g, wg0[:, 2048 * g : 2048 * (g + 1)])
+            for g in range(2):
+                interleave_w(nc.scalar, 1, g, wg1[:, 2048 * g : 2048 * (g + 1)])
+            interleave_w(nc.scalar, 2, 1, wg21[:])
+            quant_x(0)
+            quant_w(0, 0, 2, wg0[:])
+            quant_x(1)
             nc.vector.tensor_scalar(
                 out=tab[:, :, 2, :], in0=tab[:, :, 1, :], scalar1=-1.0, scalar2=None, op0=MULT
             )
-            quant_w(0, wgs[0])
-            quant_w(1, wgs[1])
+            first = passes(*UNITS[0])
+            for g in range(2):
+                scale_x(COVER_TILE, g, cover[g])
+            wg20 = wg_pool.tile([P, 2048], BF16, name="wg", align_bytes=64)
+            interleave_w(nc.gpsimd, 2, 0, wg20[:])
 
+            between = {
+                (0, 0): lambda: quant_x(2),
+                (0, 1): lambda: quant_w(1, 0, 2, wg1[:]),
+                (0, 2): lambda: quant_w(2, 0, 1, wg20[:]),
+                (1, 0): lambda: quant_w(2, 1, 1, wg21[:]),
+                (1, 1): lambda: quant_x(PLANE_PAIR),
+            }
             late = []
-            for c, j in UNITS:
-                if True:
-                    u = products(c, j)
-                    if (c, j) == (0, 0):
-                        quant_w(2, wgs[2])
-                    if (c, j) in VECTOR_ADDS:
-                        late.append((c, j, u))
-                    elif (c, j) in TENSOR_ADDS:
-                        held = (c, j, u)
-                    else:
-                        add_and_store(c, j, u)
-                    if (c, j) == (1, 3):
-                        add_and_store(*held)
-                    if (c, j) in V_BEHIND:
-                        v_unit(V_BEHIND[(c, j)])
+            held = []
+            for n, (c, j) in enumerate(UNITS):
+                if (c, j) == (1, 0):
+                    prep_x_planes(PLANE_PAIR)
+                accs = passes(c, j) if n else first
+                if (c, j) in V_BEHIND:
+                    v_unit(V_BEHIND[(c, j)])
+                if held and held[0][0] <= n:
+                    tensor_add(*held.pop(0)[1:])
+                u = products(c, j, accs)
+                if (c, j) in between:
+                    between[(c, j)]()
+                if (c, j) in VECTOR_ADDS:
+                    late.append((c, j, u))
+                elif (c, j) in TENSOR_ADDS:
+                    for a in range(2):
+                        held.append((n + TENSOR_LAG, c, j, u, a))
+                else:
+                    add_and_store(c, j, u)
+            for waiting in held:
+                tensor_add(*waiting[1:])
             for c, j, u in late:
                 add_and_store(c, j, u)

@@ -44,7 +44,7 @@ def tile_groupedqueryattention_pa_kernel(
         xv = x_bytes.rearrange("o (p i) k -> p (o i) k", i=NT)
         xb = []
         for j in range(NT // 2):
-            xb.append(const.tile([P, 2, E], U8, name="xbytes%d" % j))
+            xb.append(const.tile([P, 2, E], U8, name="xbytes%d" % j, align_bytes=256))
 
         def load_x(j):
             nc.sync.dma_start(out=xb[j][:], in_=xv[:, 2 * j : 2 * j + 2, :])
@@ -58,7 +58,7 @@ def tile_groupedqueryattention_pa_kernel(
         wraw = {}
         for c in range(3):
             for g in range(2):
-                wraw[(c, g)] = const.tile([P, 4, 512], BF16, name="wraw%d%d" % (c, g))
+                wraw[(c, g)] = const.tile([P, 4, 512], BF16, name="wraw%d%d" % (c, g), align_bytes=256)
 
         def load_w(c, g):
             if c < 2:
@@ -78,7 +78,7 @@ def tile_groupedqueryattention_pa_kernel(
         load_w(1, 0)
         load_w(1, 1)
         load_w(2, 0)
-        tab = const.tile([P, NT, 4, HALF], BF16, name="tab")
+        tab = const.tile([P, NT, 4, HALF], BF16, name="tab", align_bytes=256)
         cos_v = rope_cos.rearrange("o (p i) f -> p (o i) f", i=NT)
         sin_v = rope_sin.rearrange("o (p i) f -> p (o i) f", i=NT)
         nc.sync.dma_start(out=tab[:, :, 1, :], in_=sin_v)
@@ -187,9 +187,9 @@ def tile_groupedqueryattention_pa_kernel(
 
         q_res = []
         for c in range(2):
-            q_res.append(const.tile([P, 4, NT, P], F32, name="q_res%d" % c))
-        k_res = const.tile([P, 2, NT, P], F32, name="k_res")
-        v_res = const.tile([P, 2, NT, P], F32, name="v_res")
+            q_res.append(const.tile([P, 4, NT, P], F32, name="q_res%d" % c, align_bytes=256))
+        k_res = const.tile([P, 2, NT, P], F32, name="k_res", align_bytes=256)
+        v_res = const.tile([P, 2, NT, P], F32, name="v_res", align_bytes=256)
         q_out = out_0.rearrange("o h (p i) d -> p (o h) i d", i=NT)
         k_out = out_1.rearrange("o h (p i) d -> p (o h) i d", i=NT)
         v_out = out_2.rearrange("o h (p i) d -> p (o h) i d", i=NT)

@@ -56,20 +56,24 @@ def tile_groupedqueryattention_pa_kernel(
         for w in (Wq, Wk, Wv):
             w_views.append(w.rearrange("(g p j) w -> g p j w", p=P, j=4))
         wraw = {}
-        for c in range(3):
-            for g in range(2):
-                wraw[(c, g)] = const.tile([P, 4, 512], BF16, name="wraw%d%d" % (c, g), align_bytes=256)
+        for g in range(2):
+            for c in range(2):
+                wraw[(c, g)] = [const.tile([P, 4, 512], BF16, name="wraw%d%d" % (c, g), align_bytes=256)]
+            wraw[(2, g)] = [
+                const.tile([P, 4, 256], BF16, name="wk%d" % g, align_bytes=256),
+                const.tile([P, 4, 256], BF16, name="wv%d" % g, align_bytes=256),
+            ]
 
         def load_w(c, g):
             if c < 2:
-                nc.sync.dma_start(out=wraw[(c, g)][:], in_=w_views[0][g][:, :, 512 * c : 512 * (c + 1)])
+                nc.sync.dma_start(out=wraw[(c, g)][0][:], in_=w_views[0][g][:, :, 512 * c : 512 * (c + 1)])
             else:
-                nc.sync.dma_start(out=wraw[(c, g)][:, :, 0:256], in_=w_views[1][g])
-                nc.sync.dma_start(out=wraw[(c, g)][:, :, 256:512], in_=w_views[2][g])
+                nc.sync.dma_start(out=wraw[(c, g)][0][:], in_=w_views[1][g])
+                nc.sync.dma_start(out=wraw[(c, g)][1][:], in_=w_views[2][g])
 
         load_x_tile(0)
         sc4 = const.tile([P, 2, 4], F32, name="sc4")
-        nc.sync.dma_start(out=sc4[:], in_=x_scale.rearrange("o q (g p t) -> p (o q g) t", p=P, t=4))
+        nc.scalar.dma_start(out=sc4[:], in_=x_scale.rearrange("o q (g p t) -> p (o q g) t", p=P, t=4))
         load_x_tile(1)
         load_x(1)
         load_w(0, 0)
@@ -78,12 +82,9 @@ def tile_groupedqueryattention_pa_kernel(
         load_w(1, 0)
         load_w(1, 1)
         load_w(2, 0)
-        tab = const.tile([P, NT, 4, HALF], BF16, name="tab", align_bytes=256)
-        cos_v = rope_cos.rearrange("o (p i) f -> p (o i) f", i=NT)
-        sin_v = rope_sin.rearrange("o (p i) f -> p (o i) f", i=NT)
-        nc.sync.dma_start(out=tab[:, :, 1, :], in_=sin_v)
-        nc.sync.dma_start(out=tab[:, :, 0, :], in_=cos_v)
-        nc.sync.dma_start(out=tab[:, :, 3, :], in_=cos_v)
+        tab = const.tile([P, 3, NT, HALF], BF16, name="tab", align_bytes=256)
+        nc.sync.dma_start(out=tab[:, 2, :, :], in_=rope_sin.rearrange("o (p i) f -> p (o i) f", i=NT))
+        nc.sync.dma_start(out=tab[:, 1, :, :], in_=rope_cos.rearrange("o (p i) f -> p (o i) f", i=NT))
         load_w(2, 1)
         load_x(3)
 
@@ -108,12 +109,15 @@ def tile_groupedqueryattention_pa_kernel(
             wscl.append(const.tile([P, 1024], U8, name="wscl%d" % c, align_bytes=64))
 
         def interleave_w(engine, c, g, dst):
-            out = dst.rearrange("p (x j) -> p x j", j=4)
-            src = wraw[(c, g)][:].rearrange("p j x -> p x j")
-            if engine is nc.gpsimd:
-                nc.gpsimd.tensor_scalar(out=out, in0=src, scalar1=1.0, scalar2=0.0, op0=MULT, op1=ADD)
-            else:
-                nc.scalar.copy(out=out, in_=src)
+            pieces = wraw[(c, g)]
+            width = 2048 // len(pieces)
+            for n, piece in enumerate(pieces):
+                out = dst[:, width * n : width * (n + 1)].rearrange("p (x j) -> p x j", j=4)
+                src = piece[:].rearrange("p j x -> p x j")
+                if engine is nc.gpsimd:
+                    nc.gpsimd.tensor_scalar(out=out, in0=src, scalar1=1.0, scalar2=0.0, op0=MULT, op1=ADD)
+                else:
+                    nc.scalar.copy(out=out, in_=src)
 
         def quant_w(c, g0, passes, src):
             cols = slice(512 * g0, 512 * (g0 + passes))
@@ -227,7 +231,7 @@ def tile_groupedqueryattention_pa_kernel(
                     nc.vector.tensor_tensor(
                         out=u[:, a, b, 0:width].rearrange("p (h q e) -> p h q e", h=heads, e=2),
                         in0=y[:, :, :, b : b + 1].to_broadcast([P, heads, HALF, 2]),
-                        in1=tab[:, i, 2 * b : 2 * b + 2, :]
+                        in1=tab[:, 1 - b : 3 - b, i, :]
                         .rearrange("p e q -> p q e")
                         .unsqueeze(1)
                         .to_broadcast([P, heads, HALF, 2]),
@@ -307,7 +311,7 @@ def tile_groupedqueryattention_pa_kernel(
             quant_w(0, 0, 2, wg0[:])
             quant_x(1)
             nc.vector.tensor_scalar(
-                out=tab[:, :, 2, :], in0=tab[:, :, 1, :], scalar1=-1.0, scalar2=None, op0=MULT
+                out=tab[:, 0, :, :], in0=tab[:, 2, :, :], scalar1=-1.0, scalar2=None, op0=MULT
             )
             first = passes(*UNITS[0])
             for g in range(2):

@@ -23,6 +23,7 @@ V_BEHIND = {(1, 1): 0, (1, 2): 1, (2, 0): 2, (0, 3): 3}
 VECTOR_ADDS = ((2, 3),)
 TENSOR_ADDS = ((2, 0), (2, 1))
 COVER_TILE = 5
+WARMING = 3
 TENSOR_LAG = 2
 PLANE_PAIR = 3
 
@@ -79,12 +80,12 @@ def tile_groupedqueryattention_pa_kernel(
         load_w(0, 0)
         load_w(0, 1)
         load_x(2)
-        load_w(1, 0)
-        load_w(1, 1)
-        load_w(2, 0)
         tab = const.tile([P, 3, NT, HALF], BF16, name="tab", align_bytes=256)
         nc.sync.dma_start(out=tab[:, 2, :, :], in_=rope_sin.rearrange("o (p i) f -> p (o i) f", i=NT))
         nc.sync.dma_start(out=tab[:, 1, :, :], in_=rope_cos.rearrange("o (p i) f -> p (o i) f", i=NT))
+        load_w(1, 0)
+        load_w(1, 1)
+        load_w(2, 0)
         load_w(2, 1)
         load_x(3)
 
@@ -92,6 +93,8 @@ def tile_groupedqueryattention_pa_kernel(
         warm_out = const.tile([P, 1], F32, name="warm_out")
         nc.gpsimd.memset(warm_in[:], 0.0)
         nc.scalar.copy(out=warm_out[:], in_=warm_in[:])
+        zeros = const.tile([P, 512], BF16, name="zeros")
+        nc.gpsimd.memset(zeros[:], 0.0)
         ident = const.tile([P, P], F32, name="ident")
         make_identity(nc, ident[:])
 
@@ -126,7 +129,7 @@ def tile_groupedqueryattention_pa_kernel(
         def cast_x(i, g):
             xc = xc_pool.tile([P, 512], BF16, name="xc")
             src = xb[i // 2][:, i % 2, 512 * g : 512 * (g + 1)].bitcast(FP8)
-            if (i, g) == (0, 0):
+            if i == 0:
                 nc.vector.tensor_copy(out=xc[:], in_=src)
             else:
                 nc.scalar.copy(out=xc[:], in_=src)
@@ -191,9 +194,9 @@ def tile_groupedqueryattention_pa_kernel(
 
         q_res = []
         for c in range(2):
-            q_res.append(const.tile([P, 4, NT, P], F32, name="q_res%d" % c, align_bytes=256))
-        k_res = const.tile([P, 2, NT, P], F32, name="k_res", align_bytes=256)
-        v_res = const.tile([P, 2, NT, P], F32, name="v_res", align_bytes=256)
+            q_res.append(const.tile([P, NT // 2, 4, 2, P], F32, name="q_res%d" % c, align_bytes=256))
+        k_res = const.tile([P, NT // 2, 2, 2, P], F32, name="k_res", align_bytes=256)
+        v_res = const.tile([P, NT // 2, 2, 2, P], F32, name="v_res", align_bytes=256)
         q_out = out_0.rearrange("o h (p i) d -> p (o h) i d", i=NT)
         k_out = out_1.rearrange("o h (p i) d -> p (o h) i d", i=NT)
         v_out = out_2.rearrange("o h (p i) d -> p (o h) i d", i=NT)
@@ -221,15 +224,15 @@ def tile_groupedqueryattention_pa_kernel(
             heads = 4 if c < 2 else 2
             width = heads * P
             if c < 2:
-                u = u_pool.tile([P, 2, 2, 512], F32, name="u")
+                u = u_pool.tile([P, 2, 4, 2, P], F32, name="u")
             else:
-                u = uk_pool.tile([P, 2, 2, 256], F32, name="uk")
+                u = uk_pool.tile([P, 2, 2, 2, P], F32, name="uk")
             for a in range(2):
                 i = 2 * j + a
                 y = accs[a][:, 0:width].rearrange("p (h q e) -> p h q e", h=heads, e=2)
                 for b in range(2):
                     nc.vector.tensor_tensor(
-                        out=u[:, a, b, 0:width].rearrange("p (h q e) -> p h q e", h=heads, e=2),
+                        out=u[:, b, :, a, :].rearrange("p h (q e) -> p h q e", e=2),
                         in0=y[:, :, :, b : b + 1].to_broadcast([P, heads, HALF, 2]),
                         in1=tab[:, 1 - b : 3 - b, i, :]
                         .rearrange("p e q -> p q e")
@@ -255,47 +258,38 @@ def tile_groupedqueryattention_pa_kernel(
                     )
             rows = slice(2 * j, 2 * j + 2)
             nc.scalar.copy(
-                out=v_res[:, :, rows, :].rearrange("p h i d -> p i h d"),
+                out=v_res[:, j].rearrange("p h i d -> p i h d"),
                 in_=vacc[:].rearrange("p (i h d) -> p i h d", i=2, h=2),
             )
-            nc.sync.dma_start(out=v_out[:, :, rows, :], in_=v_res[:, :, rows, :])
+            nc.sync.dma_start(out=v_out[:, :, rows, :], in_=v_res[:, j])
 
         def tensor_add(c, j, u, a):
             i = 2 * j + a
             ksum = psum_t.tile([P, 256], F32, name="xt")
             for b in range(2):
-                nc.tensor.matmul(out=ksum[:], lhsT=ident[:], rhs=u[:, a, b, :], start=(b == 0), stop=(b == 1))
-            nc.scalar.copy(out=k_res[:, :, i, :], in_=ksum[:].rearrange("p (h d) -> p h d", h=2))
-            nc.sync.dma_start(out=k_out[:, :, i, :], in_=k_res[:, :, i, :])
+                nc.tensor.matmul(out=ksum[:], lhsT=ident[:], rhs=u[:, b, :, a, :], start=(b == 0), stop=(b == 1))
+            nc.scalar.copy(out=k_res[:, j, :, a, :], in_=ksum[:].rearrange("p (h d) -> p h d", h=2))
+            nc.sync.dma_start(out=k_out[:, :, i, :], in_=k_res[:, j, :, a, :])
 
         def add_and_store(c, j, u):
-            heads = 4 if c < 2 else 2
-            width = heads * P
             res = q_res[c] if c < 2 else k_res
             dram = q_out[:, 4 * c : 4 * c + 4] if c < 2 else k_out
             if (c, j) in VECTOR_ADDS:
                 for a in range(2):
-                    i = 2 * j + a
                     nc.vector.tensor_tensor(
-                        out=res[:, :, i, :],
-                        in0=u[:, a, 0, 0:width].rearrange("p (h d) -> p h d", h=heads),
-                        in1=u[:, a, 1, 0:width].rearrange("p (h d) -> p h d", h=heads),
-                        op=ADD,
+                        out=res[:, j, :, a, :], in0=u[:, 0, :, a, :], in1=u[:, 1, :, a, :], op=ADD
                     )
-                    nc.sync.dma_start(out=dram[:, :, i, :], in_=res[:, :, i, :])
+                    nc.sync.dma_start(out=dram[:, :, 2 * j + a, :], in_=res[:, j, :, a, :])
             else:
-                rows = slice(2 * j, 2 * j + 2)
-                nc.gpsimd.tensor_tensor(
-                    out=res[:, :, rows, :].rearrange("p h i d -> p i h d"),
-                    in0=u[:, :, 0, 0:width].rearrange("p i (h d) -> p i h d", h=heads),
-                    in1=u[:, :, 1, 0:width].rearrange("p i (h d) -> p i h d", h=heads),
-                    op=ADD,
-                )
-                nc.sync.dma_start(out=dram[:, :, rows, :], in_=res[:, :, rows, :])
+                nc.gpsimd.tensor_tensor(out=res[:, j], in0=u[:, 0], in1=u[:, 1], op=ADD)
+                nc.sync.dma_start(out=dram[:, :, 2 * j : 2 * j + 2, :], in_=res[:, j])
 
         engines = mybir.EngineType
         with tc.manual_schedule(engines={engines.DVE, engines.Activation, engines.PE, engines.Pool}):
-            for i in range(COVER_TILE):
+            turned = [turn_x(0, g) for g in range(2)]
+            for g in range(2):
+                scale_x(0, g, turned[g])
+            for i in range(1, COVER_TILE):
                 for g in range(2):
                     scale_x(i, g, turn_x(i, g))
             cover = [turn_x(COVER_TILE, g) for g in range(2)]
@@ -304,15 +298,18 @@ def tile_groupedqueryattention_pa_kernel(
             wg21 = wg_pool.tile([P, 2048], BF16, name="wg", align_bytes=64)
             for g in range(2):
                 interleave_w(nc.gpsimd, 0, g, wg0[:, 2048 * g : 2048 * (g + 1)])
+            nc.scalar.activation(
+                out=tab[:, 0, :, :], in_=tab[:, 2, :, :], func=mybir.ActivationFunctionType.Copy, scale=-1.0
+            )
             for g in range(2):
                 interleave_w(nc.scalar, 1, g, wg1[:, 2048 * g : 2048 * (g + 1)])
             interleave_w(nc.scalar, 2, 1, wg21[:])
             quant_x(0)
             quant_w(0, 0, 2, wg0[:])
             quant_x(1)
-            nc.vector.tensor_scalar(
-                out=tab[:, 0, :, :], in0=tab[:, 2, :, :], scalar1=-1.0, scalar2=None, op0=MULT
-            )
+            idle_bank = psum_a.tile([P, 512], F32, name="acc")
+            for n in range(WARMING):
+                nc.tensor.matmul(out=idle_bank[:], lhsT=zeros[:, 0:P], rhs=zeros[:], start=True, stop=True)
             first = passes(*UNITS[0])
             for g in range(2):
                 scale_x(COVER_TILE, g, cover[g])

@@ -18,14 +18,14 @@ P = 128
 E = 1024
 NT = 8
 HALF = 64
-UNITS = ((0, 0), (0, 1), (0, 2), (1, 0), (1, 1), (1, 2), (2, 0), (0, 3), (1, 3), (2, 1), (2, 2), (2, 3))
-V_BEHIND = {(1, 1): 0, (1, 2): 1, (2, 0): 2, (0, 3): 3}
+UNITS = ((0, 0), (0, 1), (1, 0), (1, 1), (2, 0), (0, 2), (1, 2), (0, 3), (1, 3), (2, 1), (2, 2), (2, 3))
+V_BEHIND = {(0, 2): 0, (1, 2): 1, (0, 3): 2, (1, 3): 3}
 VECTOR_ADDS = ((2, 3),)
 TENSOR_ADDS = ((2, 0), (2, 1))
-COVER_TILE = 5
+COVER_TILE = 4
 WARMING = 3
 TENSOR_LAG = 2
-PLANE_PAIR = 3
+PLANES_AHEAD = {(1, 0): (5,), (2, 0): (6, 7)}
 
 
 def tile_groupedqueryattention_pa_kernel(
@@ -36,6 +36,7 @@ def tile_groupedqueryattention_pa_kernel(
         const = ctx.enter_context(tc.tile_pool(name="const", bufs=1))
         xc_pool = ctx.enter_context(tc.tile_pool(name="xc_pool", bufs=6))
         wg_pool = ctx.enter_context(tc.tile_pool(name="wg_pool", bufs=3))
+        half_pool = ctx.enter_context(tc.tile_pool(name="half_pool", bufs=2))
         u_pool = ctx.enter_context(tc.tile_pool(name="u_pool", bufs=5))
         plane_pool = ctx.enter_context(tc.tile_pool(name="plane_pool", bufs=2))
         uk_pool = ctx.enter_context(tc.tile_pool(name="uk_pool", bufs=4))
@@ -111,32 +112,31 @@ def tile_groupedqueryattention_pa_kernel(
             wcodes.append(const.tile([P, 1024], U32, name="wcodes%d" % c, align_bytes=64))
             wscl.append(const.tile([P, 1024], U8, name="wscl%d" % c, align_bytes=64))
 
-        def interleave_w(engine, c, g, dst):
-            pieces = wraw[(c, g)]
-            width = 2048 // len(pieces)
+        def interleave_w(engine, pieces, dst):
+            width = dst.shape[1] // len(pieces)
             for n, piece in enumerate(pieces):
                 out = dst[:, width * n : width * (n + 1)].rearrange("p (x j) -> p x j", j=4)
-                src = piece[:].rearrange("p j x -> p x j")
+                src = piece.rearrange("p j x -> p x j")
                 if engine is nc.gpsimd:
                     nc.gpsimd.tensor_scalar(out=out, in0=src, scalar1=1.0, scalar2=0.0, op0=MULT, op1=ADD)
                 else:
                     nc.scalar.copy(out=out, in_=src)
 
-        def quant_w(c, g0, passes, src):
-            cols = slice(512 * g0, 512 * (g0 + passes))
+        def quant_w(c, first, last, src):
+            cols = slice(first, last)
             nc.vector.quantize_mx(out=wcodes[c][:, cols].bitcast(FP8X4), scales=wscl[c][:, cols], in_=src)
 
         def cast_x(i, g):
             xc = xc_pool.tile([P, 512], BF16, name="xc")
             src = xb[i // 2][:, i % 2, 512 * g : 512 * (g + 1)].bitcast(FP8)
-            if i == 0:
+            if i < 2:
                 nc.vector.tensor_copy(out=xc[:], in_=src)
             else:
                 nc.scalar.copy(out=xc[:], in_=src)
             return xc
 
-        def turn_x(i, g):
-            words = cast_x(i, g)[:].bitcast(F32)
+        def turn_x(i, g, xc):
+            words = xc[:].bitcast(F32)
             xt = psum_t.tile([P, 2, P], F32, name="xt")
             for u in range(2):
                 nc.tensor.transpose(xt[:, u, :], words[:, u:256:2], ident[:])
@@ -156,18 +156,19 @@ def tile_groupedqueryattention_pa_kernel(
                 op=MULT,
             )
 
-        def prep_x_planes(j):
-            planes = []
+        def scale_x_planes(tiles):
+            j, a0, n = tiles[0] // 2, tiles[0] % 2, len(tiles)
             xts = []
             for g in range(2):
-                xt = psum_t.tile([P, 2, 2, P], F32, name="xt")
-                for a in range(2):
-                    words = cast_x(2 * j + a, g)[:].bitcast(F32)
+                xt = psum_t.tile([P, 2, n, P], F32, name="xt")
+                for a, i in enumerate(tiles):
+                    words = cast_x(i, g)[:].bitcast(F32)
                     for u in range(2):
                         nc.tensor.transpose(xt[:, u, a, :], words[:, u:256:2], ident[:])
                 xts.append(xt)
+            planes = []
             for g in range(2):
-                plane = plane_pool.tile([P, 4, 2, P], BF16, name="plane")
+                plane = plane_pool.tile([P, 4, n, P], BF16, name="plane")
                 halves = (
                     xts[g][:].rearrange("p u a r -> p (u a r)").bitcast(BF16).rearrange("p (u s e) -> p u e s", u=2, e=2)
                 )
@@ -181,7 +182,7 @@ def tile_groupedqueryattention_pa_kernel(
                 planes.append(plane)
             for g in range(2):
                 nc.scalar.copy(
-                    out=grouped[j][:, :, 512 * g : 512 * (g + 1)].rearrange("p a (r t) -> p a r t", t=4),
+                    out=grouped[j][:, a0 : a0 + n, 512 * g : 512 * (g + 1)].rearrange("p a (r t) -> p a r t", t=4),
                     in_=planes[g][:].rearrange("p t a r -> p a r t"),
                 )
 
@@ -286,26 +287,30 @@ def tile_groupedqueryattention_pa_kernel(
 
         engines = mybir.EngineType
         with tc.manual_schedule(engines={engines.DVE, engines.Activation, engines.PE, engines.Pool}):
-            turned = [turn_x(0, g) for g in range(2)]
-            for g in range(2):
-                scale_x(0, g, turned[g])
-            for i in range(1, COVER_TILE):
+            early = {(i, g): cast_x(i, g) for i in range(2) for g in range(2)}
+            for i in range(COVER_TILE):
                 for g in range(2):
-                    scale_x(i, g, turn_x(i, g))
-            cover = [turn_x(COVER_TILE, g) for g in range(2)]
-            wg0 = wg_pool.tile([P, 4096], BF16, name="wg", align_bytes=64)
+                    xc = early[(i, g)] if i < 2 else cast_x(i, g)
+                    scale_x(i, g, turn_x(i, g, xc))
+            wg00 = wg_pool.tile([P, 2048], BF16, name="wg", align_bytes=64)
+            wg01a = half_pool.tile([P, 1024], BF16, name="wh", align_bytes=64)
+            wg01b = half_pool.tile([P, 1024], BF16, name="wh", align_bytes=64)
             wg1 = wg_pool.tile([P, 4096], BF16, name="wg", align_bytes=64)
             wg21 = wg_pool.tile([P, 2048], BF16, name="wg", align_bytes=64)
-            for g in range(2):
-                interleave_w(nc.gpsimd, 0, g, wg0[:, 2048 * g : 2048 * (g + 1)])
+            interleave_w(nc.gpsimd, [wraw[(0, 0)][0][:]], wg00[:])
+            interleave_w(nc.gpsimd, [wraw[(0, 1)][0][:, :, 0:256]], wg01a[:])
+            interleave_w(nc.scalar, [wraw[(0, 1)][0][:, :, 256:512]], wg01b[:])
+            cover = [turn_x(COVER_TILE, g, cast_x(COVER_TILE, g)) for g in range(2)]
             nc.scalar.activation(
                 out=tab[:, 0, :, :], in_=tab[:, 2, :, :], func=mybir.ActivationFunctionType.Copy, scale=-1.0
             )
             for g in range(2):
-                interleave_w(nc.scalar, 1, g, wg1[:, 2048 * g : 2048 * (g + 1)])
-            interleave_w(nc.scalar, 2, 1, wg21[:])
+                interleave_w(nc.scalar, [wraw[(1, g)][0][:]], wg1[:, 2048 * g : 2048 * (g + 1)])
+            interleave_w(nc.scalar, [piece[:] for piece in wraw[(2, 1)]], wg21[:])
             quant_x(0)
-            quant_w(0, 0, 2, wg0[:])
+            quant_w(0, 0, 512, wg00[:])
+            quant_w(0, 768, 1024, wg01b[:])
+            quant_w(0, 512, 768, wg01a[:])
             quant_x(1)
             idle_bank = psum_a.tile([P, 512], F32, name="acc")
             for n in range(WARMING):
@@ -313,21 +318,21 @@ def tile_groupedqueryattention_pa_kernel(
             first = passes(*UNITS[0])
             for g in range(2):
                 scale_x(COVER_TILE, g, cover[g])
-            wg20 = wg_pool.tile([P, 2048], BF16, name="wg", align_bytes=64)
-            interleave_w(nc.gpsimd, 2, 0, wg20[:])
+            wg20 = half_pool.tile([P, 2048], BF16, name="wh", align_bytes=64)
+            interleave_w(nc.gpsimd, [piece[:] for piece in wraw[(2, 0)]], wg20[:])
 
             between = {
-                (0, 0): lambda: quant_x(2),
-                (0, 1): lambda: quant_w(1, 0, 2, wg1[:]),
-                (0, 2): lambda: quant_w(2, 0, 1, wg20[:]),
-                (1, 0): lambda: quant_w(2, 1, 1, wg21[:]),
-                (1, 1): lambda: quant_x(PLANE_PAIR),
+                (0, 0): lambda: quant_w(1, 0, 1024, wg1[:]),
+                (0, 1): lambda: quant_w(2, 0, 512, wg20[:]),
+                (1, 0): lambda: quant_w(2, 512, 1024, wg21[:]),
+                (1, 1): lambda: quant_x(2),
+                (0, 2): lambda: quant_x(3),
             }
             late = []
             held = []
             for n, (c, j) in enumerate(UNITS):
-                if (c, j) == (1, 0):
-                    prep_x_planes(PLANE_PAIR)
+                if (c, j) in PLANES_AHEAD:
+                    scale_x_planes(PLANES_AHEAD[(c, j)])
                 accs = passes(c, j) if n else first
                 if (c, j) in V_BEHIND:
                     v_unit(V_BEHIND[(c, j)])

@@ -20,7 +20,7 @@ NT = 8
 HALF = 64
 UNITS = ((0, 0), (0, 1), (1, 0), (1, 1), (2, 0), (0, 2), (1, 2), (0, 3), (1, 3), (2, 1), (2, 2), (2, 3))
 V_BEHIND = {(0, 2): 0, (1, 2): 1, (0, 3): 2, (1, 3): 3}
-VECTOR_ADDS = ((2, 3),)
+VECTOR_ADDS = {(2, 2): 1, (2, 3): 0}
 TENSOR_ADDS = ((2, 0), (2, 1))
 COVER_TILE = 4
 WARMING = 3
@@ -272,18 +272,12 @@ def tile_groupedqueryattention_pa_kernel(
             nc.scalar.copy(out=k_res[:, j, :, a, :], in_=ksum[:].rearrange("p (h d) -> p h d", h=2))
             nc.sync.dma_start(out=k_out[:, :, i, :], in_=k_res[:, j, :, a, :])
 
-        def add_and_store(c, j, u):
+        def add_and_store(engine, c, j, u, tiles):
             res = q_res[c] if c < 2 else k_res
             dram = q_out[:, 4 * c : 4 * c + 4] if c < 2 else k_out
-            if (c, j) in VECTOR_ADDS:
-                for a in range(2):
-                    nc.vector.tensor_tensor(
-                        out=res[:, j, :, a, :], in0=u[:, 0, :, a, :], in1=u[:, 1, :, a, :], op=ADD
-                    )
-                    nc.sync.dma_start(out=dram[:, :, 2 * j + a, :], in_=res[:, j, :, a, :])
-            else:
-                nc.gpsimd.tensor_tensor(out=res[:, j], in0=u[:, 0], in1=u[:, 1], op=ADD)
-                nc.sync.dma_start(out=dram[:, :, 2 * j : 2 * j + 2, :], in_=res[:, j])
+            rows = slice(2 * j + tiles.start, 2 * j + tiles.stop)
+            engine.tensor_tensor(out=res[:, j, :, tiles, :], in0=u[:, 0, :, tiles, :], in1=u[:, 1, :, tiles, :], op=ADD)
+            nc.sync.dma_start(out=dram[:, :, rows, :], in_=res[:, j, :, tiles, :])
 
         engines = mybir.EngineType
         with tc.manual_schedule(engines={engines.DVE, engines.Activation, engines.PE, engines.Pool}):
@@ -296,7 +290,6 @@ def tile_groupedqueryattention_pa_kernel(
             wg01a = half_pool.tile([P, 1024], BF16, name="wh", align_bytes=64)
             wg01b = half_pool.tile([P, 1024], BF16, name="wh", align_bytes=64)
             wg1 = wg_pool.tile([P, 4096], BF16, name="wg", align_bytes=64)
-            wg21 = wg_pool.tile([P, 2048], BF16, name="wg", align_bytes=64)
             interleave_w(nc.gpsimd, [wraw[(0, 0)][0][:]], wg00[:])
             interleave_w(nc.gpsimd, [wraw[(0, 1)][0][:, :, 0:256]], wg01a[:])
             interleave_w(nc.scalar, [wraw[(0, 1)][0][:, :, 256:512]], wg01b[:])
@@ -306,7 +299,6 @@ def tile_groupedqueryattention_pa_kernel(
             )
             for g in range(2):
                 interleave_w(nc.scalar, [wraw[(1, g)][0][:]], wg1[:, 2048 * g : 2048 * (g + 1)])
-            interleave_w(nc.scalar, [piece[:] for piece in wraw[(2, 1)]], wg21[:])
             quant_x(0)
             quant_w(0, 0, 512, wg00[:])
             quant_w(0, 768, 1024, wg01b[:])
@@ -318,14 +310,14 @@ def tile_groupedqueryattention_pa_kernel(
             first = passes(*UNITS[0])
             for g in range(2):
                 scale_x(COVER_TILE, g, cover[g])
-            wg20 = half_pool.tile([P, 2048], BF16, name="wh", align_bytes=64)
-            interleave_w(nc.gpsimd, [piece[:] for piece in wraw[(2, 0)]], wg20[:])
+            wg2 = half_pool.tile([P, 4096], BF16, name="wh", align_bytes=64)
+            interleave_w(nc.gpsimd, [piece[:] for piece in wraw[(2, 0)]], wg2[:, 0:2048])
+            interleave_w(nc.scalar, [piece[:] for piece in wraw[(2, 1)]], wg2[:, 2048:4096])
 
             between = {
                 (0, 0): lambda: quant_w(1, 0, 1024, wg1[:]),
-                (0, 1): lambda: quant_w(2, 0, 512, wg20[:]),
-                (1, 0): lambda: quant_w(2, 512, 1024, wg21[:]),
-                (1, 1): lambda: quant_x(2),
+                (0, 1): lambda: quant_w(2, 0, 1024, wg2[:]),
+                (1, 0): lambda: quant_x(2),
                 (0, 2): lambda: quant_x(3),
             }
             late = []
@@ -341,14 +333,18 @@ def tile_groupedqueryattention_pa_kernel(
                 u = products(c, j, accs)
                 if (c, j) in between:
                     between[(c, j)]()
-                if (c, j) in VECTOR_ADDS:
-                    late.append((c, j, u))
-                elif (c, j) in TENSOR_ADDS:
+                if (c, j) in TENSOR_ADDS:
                     for a in range(2):
                         held.append((n + TENSOR_LAG, c, j, u, a))
+                elif (c, j) in VECTOR_ADDS:
+                    first_tile = VECTOR_ADDS[(c, j)]
+                    if first_tile > 0:
+                        add_and_store(nc.gpsimd, c, j, u, slice(0, first_tile))
+                    for a in range(first_tile, 2):
+                        late.append((c, j, u, slice(a, a + 1)))
                 else:
-                    add_and_store(c, j, u)
+                    add_and_store(nc.gpsimd, c, j, u, slice(0, 2))
             for waiting in held:
                 tensor_add(*waiting[1:])
-            for c, j, u in late:
-                add_and_store(c, j, u)
+            for waiting in late:
+                add_and_store(nc.vector, *waiting)

@@ -24,6 +24,7 @@ VECTOR_ADDS = {(2, 2): 1, (2, 3): 0}
 TENSOR_ADDS = ((2, 0), (2, 1))
 COVER_TILE = 4
 WARMING = 3
+LAST_Q = (1, 3)
 TENSOR_LAG = 2
 PLANES_AHEAD = {(1, 0): (5,), (2, 0): (6, 7)}
 
@@ -73,7 +74,8 @@ def tile_groupedqueryattention_pa_kernel(
                 nc.sync.dma_start(out=wraw[(c, g)][0][:], in_=w_views[1][g])
                 nc.sync.dma_start(out=wraw[(c, g)][1][:], in_=w_views[2][g])
 
-        load_x_tile(0)
+        for g in range(2):
+            nc.sync.dma_start(out=xb[0][:, 0, 512 * g : 512 * (g + 1)], in_=xv[:, 0, 512 * g : 512 * (g + 1)])
         sc4 = const.tile([P, 2, 4], F32, name="sc4")
         nc.scalar.dma_start(out=sc4[:], in_=x_scale.rearrange("o q (g p t) -> p (o q g) t", p=P, t=4))
         load_x_tile(1)
@@ -272,12 +274,14 @@ def tile_groupedqueryattention_pa_kernel(
             nc.scalar.copy(out=k_res[:, j, :, a, :], in_=ksum[:].rearrange("p (h d) -> p h d", h=2))
             nc.sync.dma_start(out=k_out[:, :, i, :], in_=k_res[:, j, :, a, :])
 
-        def add_and_store(engine, c, j, u, tiles):
+        def add_and_store(engine, c, j, u, tiles, heads=slice(None)):
             res = q_res[c] if c < 2 else k_res
             dram = q_out[:, 4 * c : 4 * c + 4] if c < 2 else k_out
             rows = slice(2 * j + tiles.start, 2 * j + tiles.stop)
-            engine.tensor_tensor(out=res[:, j, :, tiles, :], in0=u[:, 0, :, tiles, :], in1=u[:, 1, :, tiles, :], op=ADD)
-            nc.sync.dma_start(out=dram[:, :, rows, :], in_=res[:, j, :, tiles, :])
+            engine.tensor_tensor(
+                out=res[:, j, heads, tiles, :], in0=u[:, 0, heads, tiles, :], in1=u[:, 1, heads, tiles, :], op=ADD
+            )
+            nc.sync.dma_start(out=dram[:, heads, rows, :], in_=res[:, j, heads, tiles, :])
 
         engines = mybir.EngineType
         with tc.manual_schedule(engines={engines.DVE, engines.Activation, engines.PE, engines.Pool}):
@@ -342,6 +346,9 @@ def tile_groupedqueryattention_pa_kernel(
                         add_and_store(nc.gpsimd, c, j, u, slice(0, first_tile))
                     for a in range(first_tile, 2):
                         late.append((c, j, u, slice(a, a + 1)))
+                elif (c, j) == LAST_Q:
+                    for h in (0, 2):
+                        add_and_store(nc.gpsimd, c, j, u, slice(0, 2), slice(h, h + 2))
                 else:
                     add_and_store(nc.gpsimd, c, j, u, slice(0, 2))
             for waiting in held:

from contextlib import ExitStack

import concourse.mybir as mybir
from concourse.masks import make_identity

FLOPS = 2 * 1024 * 1024 * 1536

F32 = mybir.dt.float32
BF16 = mybir.dt.bfloat16
U32 = mybir.dt.uint32
U8 = mybir.dt.uint8
FP8 = mybir.dt.float8_e4m3fn
FP8X4 = mybir.dt.float8_e4m3fn_x4
MULT = mybir.AluOpType.mult
ADD = mybir.AluOpType.add

P = 128
E = 1024
NT = 8
HALF = 64
UNITS = ((0, 0), (0, 1), (1, 0), (1, 1), (2, 0), (0, 2), (1, 2), (0, 3), (1, 3), (2, 1), (2, 2), (2, 3))
V_BEHIND = {(0, 2): 0, (1, 2): 1, (0, 3): 2, (1, 3): 3}
VECTOR_ADDS = {(2, 2): 1, (2, 3): 0}
TENSOR_ADDS = ((2, 0), (2, 1))
COVER_TILE = 4
WARMING = 3
LAST_Q = (1, 3)
TENSOR_LAG = 2
PLANES_AHEAD = {(1, 0): (5,), (2, 0): (6, 7)}


def tile_groupedqueryattention_pa_kernel(
    tc, x_bytes, x_scale, rope_cos, rope_sin, Wq, Wk, Wv, out_0, out_1, out_2
):
    nc = tc.nc
    with ExitStack() as ctx:
        const = ctx.enter_context(tc.tile_pool(name="const", bufs=1))
        xc_pool = ctx.enter_context(tc.tile_pool(name="xc_pool", bufs=6))
        wg_pool = ctx.enter_context(tc.tile_pool(name="wg_pool", bufs=3))
        half_pool = ctx.enter_context(tc.tile_pool(name="half_pool", bufs=2))
        u_pool = ctx.enter_context(tc.tile_pool(name="u_pool", bufs=5))
        plane_pool = ctx.enter_context(tc.tile_pool(name="plane_pool", bufs=2))
        uk_pool = ctx.enter_context(tc.tile_pool(name="uk_pool", bufs=4))
        psum_t = ctx.enter_context(tc.psum_pool(name="psum_t", bufs=3))
        psum_a = ctx.enter_context(tc.psum_pool(name="psum_a", bufs=5))

        xv = x_bytes.rearrange("o (p i) k -> p (o i) k", i=NT)
        xb = []
        for j in range(NT // 2):
            xb.append(const.tile([P, 2, E], U8, name="xbytes%d" % j, align_bytes=256))

        def load_x(j):
            nc.sync.dma_start(out=xb[j][:], in_=xv[:, 2 * j : 2 * j + 2, :])

        def load_x_tile(i):
            nc.sync.dma_start(out=xb[i // 2][:, i % 2, :], in_=xv[:, i, :])

        w_views = []
        for w in (Wq, Wk, Wv):
            w_views.append(w.rearrange("(g p j) w -> g p j w", p=P, j=4))
        wraw = {}
        for g in range(2):
            for c in range(2):
                wraw[(c, g)] = [const.tile([P, 4, 512], BF16, name="wraw%d%d" % (c, g), align_bytes=256)]
            wraw[(2, g)] = [
                const.tile([P, 4, 256], BF16, name="wk%d" % g, align_bytes=256),
                const.tile([P, 4, 256], BF16, name="wv%d" % g, align_bytes=256),
            ]

        def load_w(c, g):
            if c < 2:
                nc.sync.dma_start(out=wraw[(c, g)][0][:], in_=w_views[0][g][:, :, 512 * c : 512 * (c + 1)])
            else:
                nc.sync.dma_start(out=wraw[(c, g)][0][:], in_=w_views[1][g])
                nc.sync.dma_start(out=wraw[(c, g)][1][:], in_=w_views[2][g])

        for g in range(2):
            nc.sync.dma_start(out=xb[0][:, 0, 512 * g : 512 * (g + 1)], in_=xv[:, 0, 512 * g : 512 * (g + 1)])
        sc4 = const.tile([P, 2, 4], F32, name="sc4")
        nc.scalar.dma_start(out=sc4[:], in_=x_scale.rearrange("o q (g p t) -> p (o q g) t", p=P, t=4))
        load_x_tile(1)
        load_x(1)
        load_w(0, 0)
        load_w(0, 1)
        load_x(2)
        tab = const.tile([P, 3, NT, HALF], BF16, name="tab", align_bytes=256)
        nc.sync.dma_start(out=tab[:, 2, :, :], in_=rope_sin.rearrange("o (p i) f -> p (o i) f", i=NT))
        nc.sync.dma_start(out=tab[:, 1, :, :], in_=rope_cos.rearrange("o (p i) f -> p (o i) f", i=NT))
        load_w(1, 0)
        load_w(1, 1)
        load_w(2, 0)
        load_w(2, 1)
        load_x(3)

        warm_in = const.tile([P, 1], F32, name="warm_in")
        warm_out = const.tile([P, 1], F32, name="warm_out")
        nc.gpsimd.memset(warm_in[:], 0.0)
        nc.scalar.copy(out=warm_out[:], in_=warm_in[:])
        zeros = const.tile([P, 512], BF16, name="zeros")
        nc.gpsimd.memset(zeros[:], 0.0)
        ident = const.tile([P, P], F32, name="ident")
        make_identity(nc, ident[:])

        grouped = []
        xcodes = []
        xscl = []
        for j in range(NT // 2):
            grouped.append(const.tile([P, 2, E], BF16, name="grouped%d" % j, align_bytes=64))
            xcodes.append(const.tile([P, 512], U32, name="xcodes%d" % j, align_bytes=64))
            xscl.append(const.tile([P, 512], U8, name="xscl%d" % j, align_bytes=64))
        wcodes = []
        wscl = []
        for c in range(3):
            wcodes.append(const.tile([P, 1024], U32, name="wcodes%d" % c, align_bytes=64))
            wscl.append(const.tile([P, 1024], U8, name="wscl%d" % c, align_bytes=64))

        def interleave_w(engine, pieces, dst):
            width = dst.shape[1] // len(pieces)
            for n, piece in enumerate(pieces):
                out = dst[:, width * n : width * (n + 1)].rearrange("p (x j) -> p x j", j=4)
                src = piece.rearrange("p j x -> p x j")
                if engine is nc.gpsimd:
                    nc.gpsimd.tensor_scalar(out=out, in0=src, scalar1=1.0, scalar2=0.0, op0=MULT, op1=ADD)
                else:
                    nc.scalar.copy(out=out, in_=src)

        def quant_w(c, first, last, src):
            cols = slice(first, last)
            nc.vector.quantize_mx(out=wcodes[c][:, cols].bitcast(FP8X4), scales=wscl[c][:, cols], in_=src)

        def cast_x(i, g):
            xc = xc_pool.tile([P, 512], BF16, name="xc")
            src = xb[i // 2][:, i % 2, 512 * g : 512 * (g + 1)].bitcast(FP8)
            if i < 2:
                nc.vector.tensor_copy(out=xc[:], in_=src)
            else:
                nc.scalar.copy(out=xc[:], in_=src)
            return xc

        def turn_x(i, g, xc):
            words = xc[:].bitcast(F32)
            xt = psum_t.tile([P, 2, P], F32, name="xt")
            for u in range(2):
                nc.tensor.transpose(xt[:, u, :], words[:, u:256:2], ident[:])
            return xt

        def scale_x(i, g, xt):
            nc.vector.tensor_tensor(
                out=grouped[i // 2][:, i % 2, 512 * g : 512 * (g + 1)].rearrange("p (r u e) -> p r u e", u=2, e=2),
                in0=xt[:]
                .rearrange("p u r -> p (u r)")
                .bitcast(BF16)
                .rearrange("p (u r e) -> p r u e", u=2, e=2),
                in1=sc4[:, g, :]
                .rearrange("p (u e) -> p u e", e=2)
                .unsqueeze(1)
                .to_broadcast([P, P, 2, 2]),
                op=MULT,
            )

        def scale_x_planes(tiles):
            j, a0, n = tiles[0] // 2, tiles[0] % 2, len(tiles)
            xts = []
            for g in range(2):
                xt = psum_t.tile([P, 2, n, P], F32, name="xt")
                for a, i in enumerate(tiles):
                    words = cast_x(i, g)[:].bitcast(F32)
                    for u in range(2):
                        nc.tensor.transpose(xt[:, u, a, :], words[:, u:256:2], ident[:])
                xts.append(xt)
            planes = []
            for g in range(2):
                plane = plane_pool.tile([P, 4, n, P], BF16, name="plane")
                halves = (
                    xts[g][:].rearrange("p u a r -> p (u a r)").bitcast(BF16).rearrange("p (u s e) -> p u e s", u=2, e=2)
                )
                for t in range(4):
                    nc.scalar.activation(
                        out=plane[:, t].rearrange("p a r -> p (a r)"),
                        in_=halves[:, t // 2, t % 2, :],
                        func=mybir.ActivationFunctionType.Copy,
                        scale=sc4[:, g, t : t + 1],
                    )
                planes.append(plane)
            for g in range(2):
                nc.scalar.copy(
                    out=grouped[j][:, a0 : a0 + n, 512 * g : 512 * (g + 1)].rearrange("p a (r t) -> p a r t", t=4),
                    in_=planes[g][:].rearrange("p t a r -> p a r t"),
                )

        def quant_x(j):
            nc.vector.quantize_mx(
                out=xcodes[j][:].bitcast(FP8X4),
                scales=xscl[j][:],
                in_=grouped[j][:].rearrange("p a n -> p (a n)"),
            )

        q_res = []
        for c in range(2):
            q_res.append(const.tile([P, NT // 2, 4, 2, P], F32, name="q_res%d" % c, align_bytes=256))
        k_res = const.tile([P, NT // 2, 2, 2, P], F32, name="k_res", align_bytes=256)
        v_res = const.tile([P, NT // 2, 2, 2, P], F32, name="v_res", align_bytes=256)
        q_out = out_0.rearrange("o h (p i) d -> p (o h) i d", i=NT)
        k_out = out_1.rearrange("o h (p i) d -> p (o h) i d", i=NT)
        v_out = out_2.rearrange("o h (p i) d -> p (o h) i d", i=NT)

        def passes(c, j):
            width = 512 if c < 2 else 256
            accs = []
            for a in range(2):
                acc = psum_a.tile([P, 512], F32, name="acc")
                for g in range(2):
                    xo = a * 256 + g * P
                    nc.tensor.matmul_mx(
                        out=acc[:, 0:width],
                        lhsT=xcodes[j][:, xo : xo + P].bitcast(FP8X4),
                        lhsT_scale=xscl[j][:, xo : xo + P],
                        rhs=wcodes[c][:, 512 * g : 512 * g + width].bitcast(FP8X4),
                        rhs_scale=wscl[c][:, 512 * g : 512 * g + width],
                        start=(g == 0),
                        stop=(g == 1),
                    )
                accs.append(acc)
            return accs

        def products(c, j, accs):
            heads = 4 if c < 2 else 2
            width = heads * P
            if c < 2:
                u = u_pool.tile([P, 2, 4, 2, P], F32, name="u")
            else:
                u = uk_pool.tile([P, 2, 2, 2, P], F32, name="uk")
            for a in range(2):
                i = 2 * j + a
                y = accs[a][:, 0:width].rearrange("p (h q e) -> p h q e", h=heads, e=2)
                for b in range(2):
                    nc.vector.tensor_tensor(
                        out=u[:, b, :, a, :].rearrange("p h (q e) -> p h q e", e=2),
                        in0=y[:, :, :, b : b + 1].to_broadcast([P, heads, HALF, 2]),
                        in1=tab[:, 1 - b : 3 - b, i, :]
                        .rearrange("p e q -> p q e")
                        .unsqueeze(1)
                        .to_broadcast([P, heads, HALF, 2]),
                        op=MULT,
                    )
            return u

        def v_unit(j):
            vacc = psum_a.tile([P, 512], F32, name="acc")
            for a in range(2):
                for g in range(2):
                    xo = a * 256 + g * P
                    nc.tensor.matmul_mx(
                        out=vacc[:, 256 * a : 256 * (a + 1)],
                        lhsT=xcodes[j][:, xo : xo + P].bitcast(FP8X4),
                        lhsT_scale=xscl[j][:, xo : xo + P],
                        rhs=wcodes[2][:, 512 * g + 256 : 512 * (g + 1)].bitcast(FP8X4),
                        rhs_scale=wscl[2][:, 512 * g + 256 : 512 * (g + 1)],
                        start=(g == 0),
                        stop=(g == 1),
                    )
            rows = slice(2 * j, 2 * j + 2)
            nc.scalar.copy(
                out=v_res[:, j].rearrange("p h i d -> p i h d"),
                in_=vacc[:].rearrange("p (i h d) -> p i h d", i=2, h=2),
            )
            nc.sync.dma_start(out=v_out[:, :, rows, :], in_=v_res[:, j])

        def tensor_add(c, j, u, a):
            i = 2 * j + a
            ksum = psum_t.tile([P, 256], F32, name="xt")
            for b in range(2):
                nc.tensor.matmul(out=ksum[:], lhsT=ident[:], rhs=u[:, b, :, a, :], start=(b == 0), stop=(b == 1))
            nc.scalar.copy(out=k_res[:, j, :, a, :], in_=ksum[:].rearrange("p (h d) -> p h d", h=2))
            nc.sync.dma_start(out=k_out[:, :, i, :], in_=k_res[:, j, :, a, :])

        def add_and_store(engine, c, j, u, tiles, heads=slice(None)):
            res = q_res[c] if c < 2 else k_res
            dram = q_out[:, 4 * c : 4 * c + 4] if c < 2 else k_out
            rows = slice(2 * j + tiles.start, 2 * j + tiles.stop)
            engine.tensor_tensor(
                out=res[:, j, heads, tiles, :], in0=u[:, 0, heads, tiles, :], in1=u[:, 1, heads, tiles, :], op=ADD
            )
            nc.sync.dma_start(out=dram[:, heads, rows, :], in_=res[:, j, heads, tiles, :])

        engines = mybir.EngineType
        with tc.manual_schedule(engines={engines.DVE, engines.Activation, engines.PE, engines.Pool}):
            early = {(i, g): cast_x(i, g) for i in range(2) for g in range(2)}
            for i in range(COVER_TILE):
                for g in range(2):
                    xc = early[(i, g)] if i < 2 else cast_x(i, g)
                    scale_x(i, g, turn_x(i, g, xc))
            wg00 = wg_pool.tile([P, 2048], BF16, name="wg", align_bytes=64)
            wg01a = half_pool.tile([P, 1024], BF16, name="wh", align_bytes=64)
            wg01b = half_pool.tile([P, 1024], BF16, name="wh", align_bytes=64)
            wg1 = wg_pool.tile([P, 4096], BF16, name="wg", align_bytes=64)
            interleave_w(nc.gpsimd, [wraw[(0, 0)][0][:]], wg00[:])
            interleave_w(nc.gpsimd, [wraw[(0, 1)][0][:, :, 0:256]], wg01a[:])
            interleave_w(nc.scalar, [wraw[(0, 1)][0][:, :, 256:512]], wg01b[:])
            cover = [turn_x(COVER_TILE, g, cast_x(COVER_TILE, g)) for g in range(2)]
            nc.scalar.activation(
                out=tab[:, 0, :, :], in_=tab[:, 2, :, :], func=mybir.ActivationFunctionType.Copy, scale=-1.0
            )
            for g in range(2):
                interleave_w(nc.scalar, [wraw[(1, g)][0][:]], wg1[:, 2048 * g : 2048 * (g + 1)])
            quant_x(0)
            quant_w(0, 0, 512, wg00[:])
            quant_w(0, 768, 1024, wg01b[:])
            quant_w(0, 512, 768, wg01a[:])
            quant_x(1)
            idle_bank = psum_a.tile([P, 512], F32, name="acc")
            for n in range(WARMING):
                nc.tensor.matmul(out=idle_bank[:], lhsT=zeros[:, 0:P], rhs=zeros[:], start=True, stop=True)
            first = passes(*UNITS[0])
            for g in range(2):
                scale_x(COVER_TILE, g, cover[g])
            wg2 = half_pool.tile([P, 4096], BF16, name="wh", align_bytes=64)
            interleave_w(nc.gpsimd, [piece[:] for piece in wraw[(2, 0)]], wg2[:, 0:2048])
            interleave_w(nc.scalar, [piece[:] for piece in wraw[(2, 1)]], wg2[:, 2048:4096])

            between = {
                (0, 0): lambda: quant_w(1, 0, 1024, wg1[:]),
                (0, 1): lambda: quant_w(2, 0, 1024, wg2[:]),
                (1, 0): lambda: quant_x(2),
                (0, 2): lambda: quant_x(3),
            }
            late = []
            held = []
            for n, (c, j) in enumerate(UNITS):
                if (c, j) in PLANES_AHEAD:
                    scale_x_planes(PLANES_AHEAD[(c, j)])
                accs = passes(c, j) if n else first
                if (c, j) in V_BEHIND:
                    v_unit(V_BEHIND[(c, j)])
                if held and held[0][0] <= n:
                    tensor_add(*held.pop(0)[1:])
                u = products(c, j, accs)
                if (c, j) in between:
                    between[(c, j)]()
                if (c, j) in TENSOR_ADDS:
                    for a in range(2):
                        held.append((n + TENSOR_LAG, c, j, u, a))
                elif (c, j) in VECTOR_ADDS:
                    first_tile = VECTOR_ADDS[(c, j)]
                    if first_tile > 0:
                        add_and_store(nc.gpsimd, c, j, u, slice(0, first_tile))
                    for a in range(first_tile, 2):
                        late.append((c, j, u, slice(a, a + 1)))
                elif (c, j) == LAST_Q:
                    for h in (0, 2):
                        add_and_store(nc.gpsimd, c, j, u, slice(0, 2), slice(h, h + 2))
                else:
                    add_and_store(nc.gpsimd, c, j, u, slice(0, 2))
            for waiting in held:
                tensor_add(*waiting[1:])
            for waiting in late:
                add_and_store(nc.vector, *waiting)
